import numpy as np
import ml_dtypes


def mxq(x, axis, fmt="e4m3"):
    dtype, down = {"e4m3": (ml_dtypes.float8_e4m3fn, 7), "e5m2": (ml_dtypes.float8_e5m2, 14)}[fmt]
    v = np.moveaxis(np.asarray(x, np.float32).astype(ml_dtypes.bfloat16).astype(np.float64), axis, -1)
    blocks = v.reshape(v.shape[:-1] + (-1, 32))
    amax = np.abs(blocks).max(-1, keepdims=True)
    byte = np.maximum(np.where(amax > 0, np.frexp(amax)[1] - 1 + 127, 0) - down, 1)
    scale = np.exp2(byte - 127.0)
    codes = (blocks / scale).astype(np.float32).astype(dtype).astype(np.float64)
    return np.moveaxis((codes * scale).reshape(v.shape), -1, axis)


WIDE = False


def mx_kscale(k):
    if not WIDE:
        return np.ones(k)
    levels = np.array([20, -20, 10, -10, 0])
    a = np.random.permutation(np.resize(levels, k // 512 * 4)).reshape(k // 512, 4)
    idx = np.arange(k)
    return np.exp2(a[idx // 512, idx % 128 // 32])


BF16 = ml_dtypes.bfloat16


def bf(x):
    return np.asarray(x, np.float32).astype(BF16)


def f64(x):
    return np.asarray(x).astype(np.float64)


B, T, D, H = 8, 256, 1024, 512


def sigmoid(v):
    return 1.0 / (1.0 + np.exp(-v))


def setup_inputs():
    u = mx_kscale(H)
    x = bf(np.random.standard_normal((B, T, D)))
    Wq0 = bf(np.random.standard_normal((H, D)) * 1.0 / np.sqrt(D))
    bq = bf(np.random.standard_normal(H) * 0.5)
    Wk0 = bf(np.random.standard_normal((H, D)) * 0.6 / np.sqrt(D))
    bk = bf(np.random.standard_normal(H) * 0.3)
    Wv0 = bf(np.random.standard_normal((H, D)) * 2.0 / np.sqrt(D))
    bv = bf(np.random.standard_normal(H) * 0.5)
    wbias = bf(np.random.uniform(0.0, 1.0, H))
    g = bf(np.random.standard_normal((B, T, H)) * np.exp2(np.random.randint(-12, 1, (B, T, 1))) * 32.0 * u)
    Q = f64(x) @ f64(Wq0).T + f64(bq)
    K = f64(x) @ f64(Wk0).T + f64(bk)
    V = f64(x) @ f64(Wv0).T + f64(bv)
    numer = np.exp(K + f64(wbias))
    P = numer / numer.sum(axis=0)
    return {"x": x,
            "Wq": bf(f64(Wq0) / u[:, None]),
            "bq": bq,
            "Wk": bf(f64(Wk0) / u[:, None]),
            "bk": bk,
            "Wv": bf(f64(Wv0) / u[:, None]),
            "bv": bv,
            "wbias": wbias,
            "Q": np.asarray(Q, np.float32),
            "P": np.asarray(P, np.float32),
            "V": np.asarray(V, np.float32),
            "grad_out": g}


def reference(x, Wq, bq, Wk, bk, Wv, bv, wbias, Q, P, V, grad_out):
    g = f64(grad_out)
    sq = sigmoid(f64(Q))
    p = f64(P)
    v = f64(V)
    weighted = (p * v).sum(axis=0)
    dw = (g * sq).sum(axis=0)
    dQ = g * weighted * sq * (1.0 - sq)
    dK = p * (v - weighted) * dw
    dV = p * dw
    gx = mxq(dQ, 2, "e5m2") @ mxq(f64(Wq), 0, "e4m3")
    gx = gx + (mxq(dK, 2, "e5m2") @ mxq(f64(Wk), 0, "e4m3"))
    gx = gx + (mxq(dV, 2, "e5m2") @ mxq(f64(Wv), 0, "e4m3"))
    return gx

@@ -1,0 +1,193 @@
+from contextlib import ExitStack
+
+import concourse.mybir as mybir
+from concourse.masks import make_identity
+
+F32 = mybir.dt.float32
+BF16 = mybir.dt.bfloat16
+U32 = mybir.dt.uint32
+U8 = mybir.dt.uint8
+E4M3_X4 = mybir.dt.float8_e4m3fn_x4
+E5M2_X4 = mybir.dt.float8_e5m2_x4
+ALU = mybir.AluOpType
+FUNC = mybir.ActivationFunctionType
+
+PARTS = 128
+BATCH, TIME, D_IN, FEATURES = 8, 256, 1024, 512
+N_TILES = BATCH * TIME // PARTS
+STEPS = PARTS // BATCH
+PACK = 4
+BLOCK = FEATURES // PACK
+N_MOVE = 512
+N_HALVES = D_IN // N_MOVE
+LOAD_TILES = 2
+N_PRODUCTS = 3
+
+FLOPS = 2 * N_PRODUCTS * BATCH * TIME * FEATURES * D_IN
+BYTES = BATCH * TIME * FEATURES * (3 * 4 + 2) + N_PRODUCTS * FEATURES * D_IN * 2 + BATCH * TIME * D_IN * 4
+
+
+def by_token_tile(tensor):
+    return tensor.flatten_outer_dims().rearrange("(p i) w -> p i w", i=N_TILES)
+
+
+def quantise_weight(nc, stage, weight, codes, scales):
+    raw = stage.tile([PARTS, PACK, D_IN], BF16, tag="raw")
+    nc.sync.dma_start(out=raw[:], in_=weight.rearrange("(j p) d -> p j d", p=PARTS))
+    for half in range(N_HALVES):
+        cols = slice(half * N_MOVE, (half + 1) * N_MOVE)
+        grouped = stage.tile([PARTS, N_MOVE, PACK], BF16, tag="grouped", align_bytes=64)
+        nc.scalar.copy(
+            out=grouped[:].rearrange("p (c i) j -> p c j i", i=4),
+            in_=raw[:, :, cols].rearrange("p j (c i) -> p c j i", i=4),
+        )
+        nc.vector.quantize_mx(
+            out=codes[:, cols].bitcast(E4M3_X4),
+            scales=scales[:, cols],
+            in_=grouped[:].rearrange("p d j -> p (d j)"),
+        )
+
+
+def tile_aftattention_t_v_kernel(
+    tc, x, w_q, b_q, w_k, b_k, w_v, b_v, w_bias, q_saved, p_saved, v_saved, grad_out, out
+):
+    nc = tc.nc
+    q_rows = by_token_tile(q_saved)
+    p_rows = by_token_tile(p_saved)
+    v_rows = by_token_tile(v_saved)
+    g_rows = by_token_tile(grad_out)
+    out_rows = by_token_tile(out)
+    weights = [w_q, w_k, w_v]
+
+    with ExitStack() as ctx:
+        consts = ctx.enter_context(tc.tile_pool(name="consts", bufs=1))
+        w_stage = ctx.enter_context(tc.tile_pool(name="w_stage", bufs=3))
+        loads = ctx.enter_context(tc.tile_pool(name="loads", bufs=3))
+        by_token = ctx.enter_context(tc.tile_pool(name="by_token", bufs=3))
+        by_feature = ctx.enter_context(tc.tile_pool(name="by_feature", bufs=3))
+        packed = ctx.enter_context(tc.tile_pool(name="packed", bufs=8))
+        results = ctx.enter_context(tc.tile_pool(name="results", bufs=3))
+        psum_turned = ctx.enter_context(tc.psum_pool(name="psum_turned", bufs=5))
+        psum_sums = ctx.enter_context(tc.psum_pool(name="psum_sums", bufs=1))
+        psum_out = ctx.enter_context(tc.psum_pool(name="psum_out", bufs=2))
+
+        identity = consts.tile([PARTS, PARTS], F32)
+        make_identity(nc, identity[:])
+        same_step = consts.tile([PARTS, STEPS], F32)
+        nc.vector.tensor_reduce(
+            out=same_step[:],
+            in_=identity[:].rearrange("p (b q) -> p q b", q=STEPS),
+            axis=mybir.AxisListType.X,
+            op=ALU.add,
+        )
+        minus_same_step = consts.tile([PARTS, STEPS], F32)
+        nc.vector.tensor_scalar_mul(out=minus_same_step[:], in0=same_step[:], scalar1=-1.0)
+
+        w_codes = consts.tile([PARTS, N_PRODUCTS, D_IN], U32, align_bytes=64)
+        w_scales = consts.tile([PARTS, N_PRODUCTS, D_IN], U8, align_bytes=64)
+
+        def load_group(group):
+            tiles = slice(group * LOAD_TILES, (group + 1) * LOAD_TILES)
+            q_in = loads.tile([PARTS, LOAD_TILES, FEATURES], F32)
+            nc.sync.dma_start(out=q_in[:], in_=q_rows[:, tiles, :])
+            g_in = loads.tile([PARTS, LOAD_TILES, FEATURES], BF16)
+            nc.sync.dma_start(out=g_in[:], in_=g_rows[:, tiles, :])
+            p_in = loads.tile([PARTS, LOAD_TILES, FEATURES], F32)
+            nc.sync.dma_start(out=p_in[:], in_=p_rows[:, tiles, :])
+            v_in = loads.tile([PARTS, LOAD_TILES, FEATURES], F32)
+            nc.sync.dma_start(out=v_in[:], in_=v_rows[:, tiles, :])
+            return q_in, g_in, p_in, v_in
+
+        loaded = []
+        for n in range(N_PRODUCTS):
+            loaded.append(load_group(n))
+            quantise_weight(nc, w_stage, weights[n], w_codes[:, n, :], w_scales[:, n, :])
+
+        for i in range(N_TILES):
+            group, slot = divmod(i, LOAD_TILES)
+            if slot == 0 and group >= N_PRODUCTS:
+                loaded.append(load_group(group))
+            q_in, g_in, p_in, v_in = loaded[group]
+
+            sq = by_token.tile([PARTS, FEATURES], F32)
+            nc.scalar.activation(out=sq[:], in_=q_in[:, slot, :], func=FUNC.Sigmoid)
+            gs = by_token.tile([PARTS, FEATURES], F32)
+            nc.vector.tensor_tensor(out=gs[:], in0=g_in[:, slot, :], in1=sq[:], op=ALU.mult)
+            a = by_token.tile([PARTS, FEATURES], F32)
+            nc.vector.scalar_tensor_tensor(
+                out=a[:], in0=sq[:], scalar=1.0, in1=gs[:], op0=ALU.subtract, op1=ALU.mult
+            )
+            pv = by_token.tile([PARTS, FEATURES], F32)
+            nc.vector.tensor_tensor(out=pv[:], in0=p_in[:, slot, :], in1=v_in[:, slot, :], op=ALU.mult)
+
+            sums = psum_sums.tile([PARTS, 2, PACK, STEPS], F32)
+            for j in range(PACK):
+                block = slice(j * BLOCK, (j + 1) * BLOCK)
+                nc.tensor.matmul(
+                    out=sums[:, 1, j, :], lhsT=gs[:, block], rhs=same_step[:], start=True, stop=True
+                )
+            for j in range(PACK):
+                block = slice(j * BLOCK, (j + 1) * BLOCK)
+                nc.tensor.matmul(
+                    out=sums[:, 0, j, :], lhsT=pv[:, block], rhs=minus_same_step[:], start=True, stop=True
+                )
+            a_t = psum_turned.tile([PARTS, PACK, PARTS], F32, tag="turned")
+            p_t = psum_turned.tile([PARTS, PACK, PARTS], F32, tag="turned")
+            v_t = psum_turned.tile([PARTS, PACK, PARTS], F32, tag="turned")
+            for turned, source in ((a_t, a[:]), (p_t, p_in[:, slot, :]), (v_t, v_in[:, slot, :])):
+                for j in range(PACK):
+                    nc.tensor.transpose(turned[:, j, :], source[:, j * BLOCK : (j + 1) * BLOCK], identity[:])
+            per_step = by_feature.tile([PARTS, 2, STEPS, PACK], F32)
+            nc.scalar.copy(out=per_step[:], in_=sums[:].rearrange("p s j q -> p s q j"))
+
+            walk = [PARTS, BATCH, STEPS, PACK]
+            minus_weighted = per_step[:, 0].unsqueeze(1).to_broadcast(walk)
+            dw = per_step[:, 1].unsqueeze(1).to_broadcast(walk)
+
+            def words_of(flat):
+                return flat.rearrange("p (b q j) -> p b q j", b=BATCH, q=STEPS)
+
+            def blocks_of(turned):
+                return turned[:].rearrange("p j (b q) -> p b q j", b=BATCH)
+
+            grads = by_feature.tile([PARTS, N_PRODUCTS * FEATURES], BF16, align_bytes=64)
+            d_q = grads[:, 0:FEATURES]
+            d_k = grads[:, FEATURES : 2 * FEATURES]
+            d_v = grads[:, 2 * FEATURES : 3 * FEATURES]
+            nc.vector.tensor_tensor(out=words_of(d_q), in0=blocks_of(a_t), in1=minus_weighted, op=ALU.mult)
+            d_v_f32 = by_feature.tile([PARTS, FEATURES], F32)
+            nc.vector.tensor_tensor(out=words_of(d_v_f32[:]), in0=blocks_of(p_t), in1=dw, op=ALU.mult)
+            nc.scalar.copy(out=d_v, in_=d_v_f32[:])
+            centred = by_feature.tile([PARTS, FEATURES], F32)
+            nc.vector.tensor_tensor(out=words_of(centred[:]), in0=blocks_of(v_t), in1=minus_weighted, op=ALU.add)
+            nc.vector.tensor_tensor(out=d_k, in0=d_v_f32[:], in1=centred[:], op=ALU.mult)
+
+            codes = packed.tile([PARTS, N_PRODUCTS * PARTS], U32, align_bytes=64)
+            scales = packed.tile([PARTS, N_PRODUCTS * PARTS], U8, align_bytes=64)
+            nc.vector.quantize_mx(
+                out=codes[:, 0 : 2 * PARTS].bitcast(E5M2_X4),
+                scales=scales[:, 0 : 2 * PARTS],
+                in_=grads[:, 0 : 2 * FEATURES],
+            )
+            nc.vector.quantize_mx(
+                out=codes[:, 2 * PARTS : 3 * PARTS].bitcast(E5M2_X4),
+                scales=scales[:, 2 * PARTS : 3 * PARTS],
+                in_=d_v,
+            )
+            result = results.tile([PARTS, D_IN], F32)
+            for half in range(N_HALVES):
+                cols = slice(half * N_MOVE, (half + 1) * N_MOVE)
+                acc = psum_out.tile([PARTS, N_MOVE], F32)
+                for n in range(N_PRODUCTS):
+                    tokens = slice(n * PARTS, (n + 1) * PARTS)
+                    nc.tensor.matmul_mx(
+                        out=acc[:],
+                        lhsT=codes[:, tokens].bitcast(E5M2_X4),
+                        lhsT_scale=scales[:, tokens],
+                        rhs=w_codes[:, n, cols].bitcast(E4M3_X4),
+                        rhs_scale=w_scales[:, n, cols],
+                        start=(n == 0),
+                        stop=(n == N_PRODUCTS - 1),
+                    )
+                nc.scalar.copy(out=result[:, cols], in_=acc[:])
+            nc.scalar.dma_start(out=out_rows[:, i, :], in_=result[:])

@@ -20,7 +20,7 @@ PACK = 4
 BLOCK = FEATURES // PACK
 N_MOVE = 512
 N_HALVES = D_IN // N_MOVE
-LOAD_TILES = 2
+LOADS_AHEAD = 8
 N_PRODUCTS = 3
 
 FLOPS = 2 * N_PRODUCTS * BATCH * TIME * FEATURES * D_IN
@@ -29,23 +29,6 @@ BYTES = BATCH * TIME * FEATURES * (3 * 4 + 2) + N_PRODUCTS * FEATURES * D_IN * 2
 
 def by_token_tile(tensor):
     return tensor.flatten_outer_dims().rearrange("(p i) w -> p i w", i=N_TILES)
-
-
-def quantise_weight(nc, stage, weight, codes, scales):
-    raw = stage.tile([PARTS, PACK, D_IN], BF16, tag="raw")
-    nc.sync.dma_start(out=raw[:], in_=weight.rearrange("(j p) d -> p j d", p=PARTS))
-    for half in range(N_HALVES):
-        cols = slice(half * N_MOVE, (half + 1) * N_MOVE)
-        grouped = stage.tile([PARTS, N_MOVE, PACK], BF16, tag="grouped", align_bytes=64)
-        nc.scalar.copy(
-            out=grouped[:].rearrange("p (c i) j -> p c j i", i=4),
-            in_=raw[:, :, cols].rearrange("p j (c i) -> p c j i", i=4),
-        )
-        nc.vector.quantize_mx(
-            out=codes[:, cols].bitcast(E4M3_X4),
-            scales=scales[:, cols],
-            in_=grouped[:].rearrange("p d j -> p (d j)"),
-        )
 
 
 def tile_aftattention_t_v_kernel(
@@ -60,16 +43,25 @@ def tile_aftattention_t_v_kernel(
     weights = [w_q, w_k, w_v]
 
     with ExitStack() as ctx:
+        ctx.enter_context(tc.manual_schedule())
         consts = ctx.enter_context(tc.tile_pool(name="consts", bufs=1))
-        w_stage = ctx.enter_context(tc.tile_pool(name="w_stage", bufs=3))
-        loads = ctx.enter_context(tc.tile_pool(name="loads", bufs=3))
+        w_stage = ctx.enter_context(tc.tile_pool(name="w_stage", bufs=N_PRODUCTS))
+        loads = ctx.enter_context(tc.tile_pool(name="loads", bufs=LOADS_AHEAD))
         by_token = ctx.enter_context(tc.tile_pool(name="by_token", bufs=3))
         by_feature = ctx.enter_context(tc.tile_pool(name="by_feature", bufs=3))
-        packed = ctx.enter_context(tc.tile_pool(name="packed", bufs=8))
+        packed = ctx.enter_context(tc.tile_pool(name="packed", bufs=3))
         results = ctx.enter_context(tc.tile_pool(name="results", bufs=3))
         psum_turned = ctx.enter_context(tc.psum_pool(name="psum_turned", bufs=5))
         psum_sums = ctx.enter_context(tc.psum_pool(name="psum_sums", bufs=1))
-        psum_out = ctx.enter_context(tc.psum_pool(name="psum_out", bufs=2))
+        psum_out = ctx.enter_context(tc.psum_pool(name="psum_out", bufs=N_HALVES))
+
+        w_codes = consts.tile([PARTS, N_PRODUCTS, D_IN], U32, align_bytes=64)
+        w_scales = consts.tile([PARTS, N_PRODUCTS, D_IN], U8, align_bytes=64)
+        w_raw = []
+        for n in range(N_PRODUCTS):
+            raw = w_stage.tile([PARTS, PACK, D_IN], BF16)
+            nc.sync.dma_start(out=raw[:], in_=weights[n].rearrange("(j p) d -> p j d", p=PARTS))
+            w_raw.append(raw)
 
         identity = consts.tile([PARTS, PARTS], F32)
         make_identity(nc, identity[:])
@@ -83,85 +75,113 @@ def tile_aftattention_t_v_kernel(
         minus_same_step = consts.tile([PARTS, STEPS], F32)
         nc.vector.tensor_scalar_mul(out=minus_same_step[:], in0=same_step[:], scalar1=-1.0)
 
-        w_codes = consts.tile([PARTS, N_PRODUCTS, D_IN], U32, align_bytes=64)
-        w_scales = consts.tile([PARTS, N_PRODUCTS, D_IN], U8, align_bytes=64)
+        def regroup(copy, grouped, raw, cols):
+            copy(
+                out=grouped[:, cols, :].rearrange("p (c i) j -> p c j i", i=4),
+                in_=raw[:, :, cols].rearrange("p j (c i) -> p c j i", i=4),
+            )
 
-        def load_group(group):
-            tiles = slice(group * LOAD_TILES, (group + 1) * LOAD_TILES)
-            q_in = loads.tile([PARTS, LOAD_TILES, FEATURES], F32)
-            nc.sync.dma_start(out=q_in[:], in_=q_rows[:, tiles, :])
-            g_in = loads.tile([PARTS, LOAD_TILES, FEATURES], BF16)
-            nc.sync.dma_start(out=g_in[:], in_=g_rows[:, tiles, :])
-            p_in = loads.tile([PARTS, LOAD_TILES, FEATURES], F32)
-            nc.sync.dma_start(out=p_in[:], in_=p_rows[:, tiles, :])
-            v_in = loads.tile([PARTS, LOAD_TILES, FEATURES], F32)
-            nc.sync.dma_start(out=v_in[:], in_=v_rows[:, tiles, :])
-            return q_in, g_in, p_in, v_in
+        w_grouped = []
+        for n in range(N_PRODUCTS + 1):
+            if n < N_PRODUCTS:
+                grouped = w_stage.tile([PARTS, D_IN, PACK], BF16, align_bytes=64)
+                regroup(nc.vector.tensor_copy, grouped, w_raw[n], slice(0, N_MOVE))
+                regroup(nc.scalar.copy, grouped, w_raw[n], slice(N_MOVE, D_IN))
+                w_grouped.append(grouped)
+            if n > 0:
+                nc.vector.quantize_mx(
+                    out=w_codes[:, n - 1, :].bitcast(E4M3_X4),
+                    scales=w_scales[:, n - 1, :],
+                    in_=w_grouped[n - 1][:].rearrange("p d j -> p (d j)"),
+                )
 
-        loaded = []
-        for n in range(N_PRODUCTS):
-            loaded.append(load_group(n))
-            quantise_weight(nc, w_stage, weights[n], w_codes[:, n, :], w_scales[:, n, :])
+        inputs, sigmoids, products, step_sums, turned, grads_of, packed_of, banks_of = {}, {}, {}, {}, {}, {}, {}, {}
 
-        for i in range(N_TILES):
-            group, slot = divmod(i, LOAD_TILES)
-            if slot == 0 and group >= N_PRODUCTS:
-                loaded.append(load_group(group))
-            q_in, g_in, p_in, v_in = loaded[group]
+        def load(i):
+            q_in = loads.tile([PARTS, FEATURES], F32)
+            nc.sync.dma_start(out=q_in[:], in_=q_rows[:, i, :])
+            g_in = loads.tile([PARTS, FEATURES], BF16)
+            nc.sync.dma_start(out=g_in[:], in_=g_rows[:, i, :])
+            p_in = loads.tile([PARTS, FEATURES], F32)
+            nc.sync.dma_start(out=p_in[:], in_=p_rows[:, i, :])
+            v_in = loads.tile([PARTS, FEATURES], F32)
+            nc.sync.dma_start(out=v_in[:], in_=v_rows[:, i, :])
+            inputs[i] = (q_in, g_in, p_in, v_in)
 
+        def sigmoid(i):
             sq = by_token.tile([PARTS, FEATURES], F32)
-            nc.scalar.activation(out=sq[:], in_=q_in[:, slot, :], func=FUNC.Sigmoid)
+            nc.scalar.activation(out=sq[:], in_=inputs[i][0][:], func=FUNC.Sigmoid)
+            sigmoids[i] = sq
+
+        def products_by_token(i):
+            q_in, g_in, p_in, v_in = inputs[i]
+            sq = sigmoids[i]
             gs = by_token.tile([PARTS, FEATURES], F32)
-            nc.vector.tensor_tensor(out=gs[:], in0=g_in[:, slot, :], in1=sq[:], op=ALU.mult)
+            nc.vector.tensor_tensor(out=gs[:], in0=g_in[:], in1=sq[:], op=ALU.mult)
+            pv = by_token.tile([PARTS, FEATURES], F32)
+            nc.vector.tensor_tensor(out=pv[:], in0=p_in[:], in1=v_in[:], op=ALU.mult)
             a = by_token.tile([PARTS, FEATURES], F32)
             nc.vector.scalar_tensor_tensor(
                 out=a[:], in0=sq[:], scalar=1.0, in1=gs[:], op0=ALU.subtract, op1=ALU.mult
             )
-            pv = by_token.tile([PARTS, FEATURES], F32)
-            nc.vector.tensor_tensor(out=pv[:], in0=p_in[:, slot, :], in1=v_in[:, slot, :], op=ALU.mult)
+            products[i] = (gs, pv, a)
 
+        def batch_sums(i):
+            gs, pv, a = products[i]
             sums = psum_sums.tile([PARTS, 2, PACK, STEPS], F32)
             for j in range(PACK):
                 block = slice(j * BLOCK, (j + 1) * BLOCK)
-                nc.tensor.matmul(
-                    out=sums[:, 1, j, :], lhsT=gs[:, block], rhs=same_step[:], start=True, stop=True
-                )
+                nc.tensor.matmul(out=sums[:, 1, j, :], lhsT=gs[:, block], rhs=same_step[:], start=True, stop=True)
             for j in range(PACK):
                 block = slice(j * BLOCK, (j + 1) * BLOCK)
                 nc.tensor.matmul(
                     out=sums[:, 0, j, :], lhsT=pv[:, block], rhs=minus_same_step[:], start=True, stop=True
                 )
-            a_t = psum_turned.tile([PARTS, PACK, PARTS], F32, tag="turned")
-            p_t = psum_turned.tile([PARTS, PACK, PARTS], F32, tag="turned")
-            v_t = psum_turned.tile([PARTS, PACK, PARTS], F32, tag="turned")
-            for turned, source in ((a_t, a[:]), (p_t, p_in[:, slot, :]), (v_t, v_in[:, slot, :])):
-                for j in range(PACK):
-                    nc.tensor.transpose(turned[:, j, :], source[:, j * BLOCK : (j + 1) * BLOCK], identity[:])
-            per_step = by_feature.tile([PARTS, 2, STEPS, PACK], F32)
+            per_step = by_feature.tile([PARTS, 2, STEPS, PACK], F32, bufs=4)
             nc.scalar.copy(out=per_step[:], in_=sums[:].rearrange("p s j q -> p s q j"))
+            step_sums[i] = per_step
 
+        def turn(i, what, source):
+            bank = psum_turned.tile([PARTS, PACK, PARTS], F32, tag="turned")
+            for j in range(PACK):
+                nc.tensor.transpose(bank[:, j, :], source[:, j * BLOCK : (j + 1) * BLOCK], identity[:])
+            turned[(i, what)] = bank
+
+        def turn_v(i):
+            turn(i, "v", inputs[i][3])
+
+        def turn_p(i):
+            turn(i, "p", inputs[i][2])
+
+        def turn_a(i):
+            turn(i, "a", products[i][2])
+
+        def products_by_feature(i):
             walk = [PARTS, BATCH, STEPS, PACK]
-            minus_weighted = per_step[:, 0].unsqueeze(1).to_broadcast(walk)
-            dw = per_step[:, 1].unsqueeze(1).to_broadcast(walk)
+            minus_weighted = step_sums[i][:, 0].unsqueeze(1).to_broadcast(walk)
+            dw = step_sums[i][:, 1].unsqueeze(1).to_broadcast(walk)
 
             def words_of(flat):
                 return flat.rearrange("p (b q j) -> p b q j", b=BATCH, q=STEPS)
 
-            def blocks_of(turned):
-                return turned[:].rearrange("p j (b q) -> p b q j", b=BATCH)
+            def blocks_of(what):
+                return turned[(i, what)][:].rearrange("p j (b q) -> p b q j", b=BATCH)
 
             grads = by_feature.tile([PARTS, N_PRODUCTS * FEATURES], BF16, align_bytes=64)
             d_q = grads[:, 0:FEATURES]
             d_k = grads[:, FEATURES : 2 * FEATURES]
             d_v = grads[:, 2 * FEATURES : 3 * FEATURES]
-            nc.vector.tensor_tensor(out=words_of(d_q), in0=blocks_of(a_t), in1=minus_weighted, op=ALU.mult)
-            d_v_f32 = by_feature.tile([PARTS, FEATURES], F32)
-            nc.vector.tensor_tensor(out=words_of(d_v_f32[:]), in0=blocks_of(p_t), in1=dw, op=ALU.mult)
-            nc.scalar.copy(out=d_v, in_=d_v_f32[:])
             centred = by_feature.tile([PARTS, FEATURES], F32)
-            nc.vector.tensor_tensor(out=words_of(centred[:]), in0=blocks_of(v_t), in1=minus_weighted, op=ALU.add)
+            nc.vector.tensor_tensor(out=words_of(centred[:]), in0=blocks_of("v"), in1=minus_weighted, op=ALU.add)
+            d_v_f32 = by_feature.tile([PARTS, FEATURES], F32)
+            nc.vector.tensor_tensor(out=words_of(d_v_f32[:]), in0=blocks_of("p"), in1=dw, op=ALU.mult)
+            nc.scalar.copy(out=d_v, in_=d_v_f32[:])
+            nc.vector.tensor_tensor(out=words_of(d_q), in0=blocks_of("a"), in1=minus_weighted, op=ALU.mult)
             nc.vector.tensor_tensor(out=d_k, in0=d_v_f32[:], in1=centred[:], op=ALU.mult)
+            grads_of[i] = grads
 
+        def quantise(i):
+            grads = grads_of[i]
             codes = packed.tile([PARTS, N_PRODUCTS * PARTS], U32, align_bytes=64)
             scales = packed.tile([PARTS, N_PRODUCTS * PARTS], U8, align_bytes=64)
             nc.vector.quantize_mx(
@@ -172,9 +192,13 @@ def tile_aftattention_t_v_kernel(
             nc.vector.quantize_mx(
                 out=codes[:, 2 * PARTS : 3 * PARTS].bitcast(E5M2_X4),
                 scales=scales[:, 2 * PARTS : 3 * PARTS],
-                in_=d_v,
+                in_=grads[:, 2 * FEATURES : 3 * FEATURES],
             )
-            result = results.tile([PARTS, D_IN], F32)
+            packed_of[i] = (codes, scales)
+
+        def multiply(i):
+            codes, scales = packed_of[i]
+            banks_of[i] = []
             for half in range(N_HALVES):
                 cols = slice(half * N_MOVE, (half + 1) * N_MOVE)
                 acc = psum_out.tile([PARTS, N_MOVE], F32)
@@ -189,5 +213,27 @@ def tile_aftattention_t_v_kernel(
                         start=(n == 0),
                         stop=(n == N_PRODUCTS - 1),
                     )
-                nc.scalar.copy(out=result[:, cols], in_=acc[:])
+                banks_of[i].append(acc)
+
+        def store(i):
+            result = results.tile([PARTS, D_IN], F32)
+            for half in range(N_HALVES):
+                nc.scalar.copy(out=result[:, half * N_MOVE : (half + 1) * N_MOVE], in_=banks_of[i][half][:])
             nc.scalar.dma_start(out=out_rows[:, i, :], in_=result[:])
+
+        def run(stage, i):
+            if 0 <= i < N_TILES:
+                stage(i)
+
+        for k in range(-LOADS_AHEAD, N_TILES + 2):
+            run(load, k + LOADS_AHEAD)
+            run(store, k - 2)
+            run(sigmoid, k + 3)
+            run(products_by_token, k + 2)
+            run(batch_sums, k + 2)
+            run(quantise, k - 1)
+            run(multiply, k - 1)
+            run(products_by_feature, k)
+            run(turn_a, k + 1)
+            run(turn_v, k + 2)
+            run(turn_p, k + 2)

@@ -15,44 +15,39 @@ FUNC = mybir.ActivationFunctionType
 PARTS = 128
 BATCH, TIME, D_IN, FEATURES = 8, 256, 1024, 512
 N_TILES = BATCH * TIME // PARTS
-STEPS = PARTS // BATCH
 PACK = 4
 BLOCK = FEATURES // PACK
 N_MOVE = 512
 N_HALVES = D_IN // N_MOVE
-LOADS_AHEAD = 8
 N_PRODUCTS = 3
+LOADS_AHEAD = 3
 
 FLOPS = 2 * N_PRODUCTS * BATCH * TIME * FEATURES * D_IN
 BYTES = BATCH * TIME * FEATURES * (3 * 4 + 2) + N_PRODUCTS * FEATURES * D_IN * 2 + BATCH * TIME * D_IN * 4
 
 
-def by_token_tile(tensor):
-    return tensor.flatten_outer_dims().rearrange("(p i) w -> p i w", i=N_TILES)
+def token_tile(tensor, i):
+    half, b = divmod(i, BATCH)
+    return tensor[b, half * PARTS : (half + 1) * PARTS, :]
 
 
 def tile_aftattention_t_v_kernel(
     tc, x, w_q, b_q, w_k, b_k, w_v, b_v, w_bias, q_saved, p_saved, v_saved, grad_out, out
 ):
     nc = tc.nc
-    q_rows = by_token_tile(q_saved)
-    p_rows = by_token_tile(p_saved)
-    v_rows = by_token_tile(v_saved)
-    g_rows = by_token_tile(grad_out)
-    out_rows = by_token_tile(out)
     weights = [w_q, w_k, w_v]
 
     with ExitStack() as ctx:
         ctx.enter_context(tc.manual_schedule())
         consts = ctx.enter_context(tc.tile_pool(name="consts", bufs=1))
         w_stage = ctx.enter_context(tc.tile_pool(name="w_stage", bufs=N_PRODUCTS))
-        loads = ctx.enter_context(tc.tile_pool(name="loads", bufs=LOADS_AHEAD))
+        loads = ctx.enter_context(tc.tile_pool(name="loads", bufs=LOADS_AHEAD + 1))
         by_token = ctx.enter_context(tc.tile_pool(name="by_token", bufs=3))
         by_feature = ctx.enter_context(tc.tile_pool(name="by_feature", bufs=3))
         packed = ctx.enter_context(tc.tile_pool(name="packed", bufs=3))
         results = ctx.enter_context(tc.tile_pool(name="results", bufs=3))
-        psum_turned = ctx.enter_context(tc.psum_pool(name="psum_turned", bufs=5))
         psum_sums = ctx.enter_context(tc.psum_pool(name="psum_sums", bufs=1))
+        psum_turned = ctx.enter_context(tc.psum_pool(name="psum_turned", bufs=4))
         psum_out = ctx.enter_context(tc.psum_pool(name="psum_out", bufs=N_HALVES))
 
         w_codes = consts.tile([PARTS, N_PRODUCTS, D_IN], U32, align_bytes=64)
@@ -65,15 +60,6 @@ def tile_aftattention_t_v_kernel(
 
         identity = consts.tile([PARTS, PARTS], F32)
         make_identity(nc, identity[:])
-        same_step = consts.tile([PARTS, STEPS], F32)
-        nc.vector.tensor_reduce(
-            out=same_step[:],
-            in_=identity[:].rearrange("p (b q) -> p q b", q=STEPS),
-            axis=mybir.AxisListType.X,
-            op=ALU.add,
-        )
-        minus_same_step = consts.tile([PARTS, STEPS], F32)
-        nc.vector.tensor_scalar_mul(out=minus_same_step[:], in0=same_step[:], scalar1=-1.0)
 
         def regroup(copy, grouped, raw, cols):
             copy(
@@ -95,17 +81,18 @@ def tile_aftattention_t_v_kernel(
                     in_=w_grouped[n - 1][:].rearrange("p d j -> p (d j)"),
                 )
 
-        inputs, sigmoids, products, step_sums, turned, grads_of, packed_of, banks_of = {}, {}, {}, {}, {}, {}, {}, {}
+        inputs, sigmoids, products, sum_banks, half_sums = {}, {}, {}, {}, {}
+        turned, grads_of, packed_of, banks_of = {}, {}, {}, {}
 
         def load(i):
             q_in = loads.tile([PARTS, FEATURES], F32)
-            nc.sync.dma_start(out=q_in[:], in_=q_rows[:, i, :])
+            nc.sync.dma_start(out=q_in[:], in_=token_tile(q_saved, i))
             g_in = loads.tile([PARTS, FEATURES], BF16)
-            nc.sync.dma_start(out=g_in[:], in_=g_rows[:, i, :])
-            p_in = loads.tile([PARTS, FEATURES], F32)
-            nc.sync.dma_start(out=p_in[:], in_=p_rows[:, i, :])
-            v_in = loads.tile([PARTS, FEATURES], F32)
-            nc.sync.dma_start(out=v_in[:], in_=v_rows[:, i, :])
+            nc.sync.dma_start(out=g_in[:], in_=token_tile(grad_out, i))
+            p_in = loads.tile([PARTS, FEATURES], F32, bufs=LOADS_AHEAD + BATCH)
+            nc.sync.dma_start(out=p_in[:], in_=token_tile(p_saved, i))
+            v_in = loads.tile([PARTS, FEATURES], F32, bufs=LOADS_AHEAD + BATCH)
+            nc.sync.dma_start(out=v_in[:], in_=token_tile(v_saved, i))
             inputs[i] = (q_in, g_in, p_in, v_in)
 
         def sigmoid(i):
@@ -114,32 +101,41 @@ def tile_aftattention_t_v_kernel(
             sigmoids[i] = sq
 
         def products_by_token(i):
-            q_in, g_in, p_in, v_in = inputs[i]
+            g_in, p_in, v_in = inputs[i][1:]
             sq = sigmoids[i]
             gs = by_token.tile([PARTS, FEATURES], F32)
             nc.vector.tensor_tensor(out=gs[:], in0=g_in[:], in1=sq[:], op=ALU.mult)
             pv = by_token.tile([PARTS, FEATURES], F32)
             nc.vector.tensor_tensor(out=pv[:], in0=p_in[:], in1=v_in[:], op=ALU.mult)
-            a = by_token.tile([PARTS, FEATURES], F32)
+            a = by_token.tile([PARTS, FEATURES], F32, bufs=BATCH + 2)
             nc.vector.scalar_tensor_tensor(
                 out=a[:], in0=sq[:], scalar=1.0, in1=gs[:], op0=ALU.subtract, op1=ALU.mult
             )
             products[i] = (gs, pv, a)
 
-        def batch_sums(i):
-            gs, pv, a = products[i]
-            sums = psum_sums.tile([PARTS, 2, PACK, STEPS], F32)
-            for j in range(PACK):
-                block = slice(j * BLOCK, (j + 1) * BLOCK)
-                nc.tensor.matmul(out=sums[:, 1, j, :], lhsT=gs[:, block], rhs=same_step[:], start=True, stop=True)
-            for j in range(PACK):
-                block = slice(j * BLOCK, (j + 1) * BLOCK)
-                nc.tensor.matmul(
-                    out=sums[:, 0, j, :], lhsT=pv[:, block], rhs=minus_same_step[:], start=True, stop=True
-                )
-            per_step = by_feature.tile([PARTS, 2, STEPS, PACK], F32, bufs=4)
-            nc.scalar.copy(out=per_step[:], in_=sums[:].rearrange("p s j q -> p s q j"))
-            step_sums[i] = per_step
+        def add_to_sums(i):
+            half, b = divmod(i, BATCH)
+            if b == 0:
+                weighted_bank = psum_sums.tile([PARTS, PACK, PARTS], F32)
+                dw_bank = psum_sums.tile([PARTS, PACK, PARTS], F32)
+                sum_banks[half] = (weighted_bank, dw_bank)
+            for bank, source in zip(sum_banks[half], (products[i][1], products[i][0])):
+                for j in range(PACK):
+                    nc.tensor.matmul(
+                        out=bank[:, j, :],
+                        lhsT=source[:, j * BLOCK : (j + 1) * BLOCK],
+                        rhs=identity[:],
+                        is_transpose=True,
+                        start=(b == 0 and j == 0),
+                        stop=(b == BATCH - 1 and j == PACK - 1),
+                    )
+            if b == BATCH - 1:
+                weighted_bank, dw_bank = sum_banks[half]
+                minus_weighted = by_feature.tile([PARTS, PARTS, PACK], F32, bufs=2)
+                nc.scalar.mul(out=minus_weighted[:], in_=weighted_bank[:].rearrange("p j t -> p t j"), mul=-1.0)
+                dw = by_feature.tile([PARTS, PARTS, PACK], F32, bufs=2)
+                nc.scalar.copy(out=dw[:], in_=dw_bank[:].rearrange("p j t -> p t j"))
+                half_sums[half] = (minus_weighted, dw)
 
         def turn(i, what, source):
             bank = psum_turned.tile([PARTS, PACK, PARTS], F32, tag="turned")
@@ -157,26 +153,24 @@ def tile_aftattention_t_v_kernel(
             turn(i, "a", products[i][2])
 
         def products_by_feature(i):
-            walk = [PARTS, BATCH, STEPS, PACK]
-            minus_weighted = step_sums[i][:, 0].unsqueeze(1).to_broadcast(walk)
-            dw = step_sums[i][:, 1].unsqueeze(1).to_broadcast(walk)
+            minus_weighted, dw = half_sums[i // BATCH]
 
             def words_of(flat):
-                return flat.rearrange("p (b q j) -> p b q j", b=BATCH, q=STEPS)
+                return flat.rearrange("p (t j) -> p t j", j=PACK)
 
             def blocks_of(what):
-                return turned[(i, what)][:].rearrange("p j (b q) -> p b q j", b=BATCH)
+                return turned[(i, what)][:].rearrange("p j t -> p t j")
 
             grads = by_feature.tile([PARTS, N_PRODUCTS * FEATURES], BF16, align_bytes=64)
             d_q = grads[:, 0:FEATURES]
             d_k = grads[:, FEATURES : 2 * FEATURES]
             d_v = grads[:, 2 * FEATURES : 3 * FEATURES]
             centred = by_feature.tile([PARTS, FEATURES], F32)
-            nc.vector.tensor_tensor(out=words_of(centred[:]), in0=blocks_of("v"), in1=minus_weighted, op=ALU.add)
+            nc.vector.tensor_tensor(out=words_of(centred[:]), in0=blocks_of("v"), in1=minus_weighted[:], op=ALU.add)
             d_v_f32 = by_feature.tile([PARTS, FEATURES], F32)
-            nc.vector.tensor_tensor(out=words_of(d_v_f32[:]), in0=blocks_of("p"), in1=dw, op=ALU.mult)
+            nc.vector.tensor_tensor(out=words_of(d_v_f32[:]), in0=blocks_of("p"), in1=dw[:], op=ALU.mult)
             nc.scalar.copy(out=d_v, in_=d_v_f32[:])
-            nc.vector.tensor_tensor(out=words_of(d_q), in0=blocks_of("a"), in1=minus_weighted, op=ALU.mult)
+            nc.vector.tensor_tensor(out=words_of(d_q), in0=blocks_of("a"), in1=minus_weighted[:], op=ALU.mult)
             nc.vector.tensor_tensor(out=d_k, in0=d_v_f32[:], in1=centred[:], op=ALU.mult)
             grads_of[i] = grads
 
@@ -219,21 +213,22 @@ def tile_aftattention_t_v_kernel(
             result = results.tile([PARTS, D_IN], F32)
             for half in range(N_HALVES):
                 nc.scalar.copy(out=result[:, half * N_MOVE : (half + 1) * N_MOVE], in_=banks_of[i][half][:])
-            nc.scalar.dma_start(out=out_rows[:, i, :], in_=result[:])
+            nc.scalar.dma_start(out=token_tile(out, i), in_=result[:])
 
         def run(stage, i):
             if 0 <= i < N_TILES:
                 stage(i)
 
-        for k in range(-LOADS_AHEAD, N_TILES + 2):
-            run(load, k + LOADS_AHEAD)
-            run(store, k - 2)
-            run(sigmoid, k + 3)
-            run(products_by_token, k + 2)
-            run(batch_sums, k + 2)
+        first_round = -(BATCH + 1 + LOADS_AHEAD)
+        for k in range(first_round, N_TILES + 1):
+            run(sigmoid, k + BATCH + 1)
+            run(products_by_token, k + BATCH)
+            run(add_to_sums, k + BATCH)
             run(quantise, k - 1)
             run(multiply, k - 1)
             run(products_by_feature, k)
+            run(store, k - 1)
+            run(turn_p, k + 1)
             run(turn_a, k + 1)
             run(turn_v, k + 2)
-            run(turn_p, k + 2)
+            run(load, k + BATCH + 1 + LOADS_AHEAD)

@@ -82,7 +82,7 @@ def tile_aftattention_t_v_kernel(
                 )
 
         inputs, sigmoids, products, sum_banks, half_sums = {}, {}, {}, {}, {}
-        turned, grads_of, packed_of, banks_of = {}, {}, {}, {}
+        turned, grads_of, packed_of, banks_of, derivatives = {}, {}, {}, {}, {}
 
         def load(i):
             q_in = loads.tile([PARTS, FEATURES], F32)
@@ -98,20 +98,26 @@ def tile_aftattention_t_v_kernel(
         def sigmoid(i):
             sq = by_token.tile([PARTS, FEATURES], F32)
             nc.scalar.activation(out=sq[:], in_=inputs[i][0][:], func=FUNC.Sigmoid)
-            sigmoids[i] = sq
+            one_minus = by_token.tile([PARTS, FEATURES], F32, bufs=BATCH + 3)
+            nc.scalar.activation(out=one_minus[:], in_=inputs[i][0][:], func=FUNC.Sigmoid, scale=-1.0)
+            sigmoids[i] = (sq, one_minus)
 
         def products_by_token(i):
             g_in, p_in, v_in = inputs[i][1:]
-            sq = sigmoids[i]
-            gs = by_token.tile([PARTS, FEATURES], F32)
+            sq = sigmoids[i][0]
+            gs = by_token.tile([PARTS, FEATURES], F32, bufs=BATCH + 2)
             nc.vector.tensor_tensor(out=gs[:], in0=g_in[:], in1=sq[:], op=ALU.mult)
             pv = by_token.tile([PARTS, FEATURES], F32)
             nc.vector.tensor_tensor(out=pv[:], in0=p_in[:], in1=v_in[:], op=ALU.mult)
-            a = by_token.tile([PARTS, FEATURES], F32, bufs=BATCH + 2)
-            nc.vector.scalar_tensor_tensor(
-                out=a[:], in0=sq[:], scalar=1.0, in1=gs[:], op0=ALU.subtract, op1=ALU.mult
-            )
-            products[i] = (gs, pv, a)
+            products[i] = (gs, pv)
+
+        def shared_slot(i, shape, dtype):
+            return by_feature.tile(shape, dtype, tag="slot%d" % (i % 2), bufs=1, align_bytes=64, name="slot")
+
+        def derivative(i):
+            a = shared_slot(i, [PARTS, FEATURES], F32)
+            nc.gpsimd.tensor_tensor(out=a[:], in0=products[i][0][:], in1=sigmoids[i][1][:], op=ALU.mult)
+            derivatives[i] = a
 
         def add_to_sums(i):
             half, b = divmod(i, BATCH)
@@ -131,11 +137,11 @@ def tile_aftattention_t_v_kernel(
                     )
             if b == BATCH - 1:
                 weighted_bank, dw_bank = sum_banks[half]
-                minus_weighted = by_feature.tile([PARTS, PARTS, PACK], F32, bufs=2)
-                nc.scalar.mul(out=minus_weighted[:], in_=weighted_bank[:].rearrange("p j t -> p t j"), mul=-1.0)
+                weighted = by_feature.tile([PARTS, PARTS, PACK], F32, bufs=2)
+                nc.scalar.copy(out=weighted[:], in_=weighted_bank[:].rearrange("p j t -> p t j"))
                 dw = by_feature.tile([PARTS, PARTS, PACK], F32, bufs=2)
                 nc.scalar.copy(out=dw[:], in_=dw_bank[:].rearrange("p j t -> p t j"))
-                half_sums[half] = (minus_weighted, dw)
+                half_sums[half] = (weighted, dw)
 
         def turn(i, what, source):
             bank = psum_turned.tile([PARTS, PACK, PARTS], F32, tag="turned")
@@ -150,10 +156,10 @@ def tile_aftattention_t_v_kernel(
             turn(i, "p", inputs[i][2])
 
         def turn_a(i):
-            turn(i, "a", products[i][2])
+            turn(i, "a", derivatives[i])
 
         def products_by_feature(i):
-            minus_weighted, dw = half_sums[i // BATCH]
+            weighted, dw = half_sums[i // BATCH]
 
             def words_of(flat):
                 return flat.rearrange("p (t j) -> p t j", j=PACK)
@@ -161,16 +167,16 @@ def tile_aftattention_t_v_kernel(
             def blocks_of(what):
                 return turned[(i, what)][:].rearrange("p j t -> p t j")
 
-            grads = by_feature.tile([PARTS, N_PRODUCTS * FEATURES], BF16, align_bytes=64)
+            grads = shared_slot(i, [PARTS, N_PRODUCTS * FEATURES], BF16)
             d_q = grads[:, 0:FEATURES]
             d_k = grads[:, FEATURES : 2 * FEATURES]
             d_v = grads[:, 2 * FEATURES : 3 * FEATURES]
             centred = by_feature.tile([PARTS, FEATURES], F32)
-            nc.vector.tensor_tensor(out=words_of(centred[:]), in0=blocks_of("v"), in1=minus_weighted[:], op=ALU.add)
+            nc.vector.tensor_tensor(out=words_of(centred[:]), in0=blocks_of("v"), in1=weighted[:], op=ALU.subtract)
             d_v_f32 = by_feature.tile([PARTS, FEATURES], F32)
             nc.vector.tensor_tensor(out=words_of(d_v_f32[:]), in0=blocks_of("p"), in1=dw[:], op=ALU.mult)
             nc.scalar.copy(out=d_v, in_=d_v_f32[:])
-            nc.vector.tensor_tensor(out=words_of(d_q), in0=blocks_of("a"), in1=minus_weighted[:], op=ALU.mult)
+            nc.vector.tensor_tensor(out=words_of(d_q), in0=blocks_of("a"), in1=weighted[:], op=ALU.mult)
             nc.vector.tensor_tensor(out=d_k, in0=d_v_f32[:], in1=centred[:], op=ALU.mult)
             grads_of[i] = grads
 
@@ -225,6 +231,7 @@ def tile_aftattention_t_v_kernel(
             run(products_by_token, k + BATCH)
             run(add_to_sums, k + BATCH)
             run(quantise, k - 1)
+            run(derivative, k + 1)
             run(multiply, k - 1)
             run(products_by_feature, k)
             run(store, k - 1)

@@ -15,6 +15,13 @@ FUNC = mybir.ActivationFunctionType
 PARTS = 128
 BATCH, TIME, D_IN, FEATURES = 8, 256, 1024, 512
 N_TILES = BATCH * TIME // PARTS
+ENTRIES = 2
+STEPS = PARTS // ENTRIES
+GROUP = BATCH // ENTRIES
+N_GROUPS = N_TILES // GROUP
+SPLIT = 2
+PART_WIDTH = FEATURES // SPLIT
+BLOCKS = PART_WIDTH // PARTS
 PACK = 4
 BLOCK = FEATURES // PACK
 N_MOVE = 512
@@ -27,8 +34,9 @@ BYTES = BATCH * TIME * FEATURES * (3 * 4 + 2) + N_PRODUCTS * FEATURES * D_IN * 2
 
 
 def token_tile(tensor, i):
-    half, b = divmod(i, BATCH)
-    return tensor[b, half * PARTS : (half + 1) * PARTS, :]
+    group, pair = divmod(i, GROUP)
+    rows = tensor[ENTRIES * pair : ENTRIES * (pair + 1), group * STEPS : (group + 1) * STEPS, :]
+    return rows.rearrange("c t (f h) -> (t f) c h", f=SPLIT)
 
 
 def tile_aftattention_t_v_kernel(
@@ -47,7 +55,7 @@ def tile_aftattention_t_v_kernel(
         packed = ctx.enter_context(tc.tile_pool(name="packed", bufs=3))
         results = ctx.enter_context(tc.tile_pool(name="results", bufs=3))
         psum_sums = ctx.enter_context(tc.psum_pool(name="psum_sums", bufs=1))
-        psum_turned = ctx.enter_context(tc.psum_pool(name="psum_turned", bufs=4))
+        psum_turned = ctx.enter_context(tc.psum_pool(name="psum_turned", bufs=5))
         psum_out = ctx.enter_context(tc.psum_pool(name="psum_out", bufs=N_HALVES))
 
         w_codes = consts.tile([PARTS, N_PRODUCTS, D_IN], U32, align_bytes=64)
@@ -84,30 +92,32 @@ def tile_aftattention_t_v_kernel(
         inputs, sigmoids, products, sum_banks, half_sums = {}, {}, {}, {}, {}
         turned, grads_of, packed_of, banks_of, derivatives = {}, {}, {}, {}, {}
 
+        BY_TOKEN = [PARTS, ENTRIES, PART_WIDTH]
+
         def load(i):
-            q_in = loads.tile([PARTS, FEATURES], F32)
+            q_in = loads.tile(BY_TOKEN, F32)
             nc.sync.dma_start(out=q_in[:], in_=token_tile(q_saved, i))
-            g_in = loads.tile([PARTS, FEATURES], BF16)
+            g_in = loads.tile(BY_TOKEN, BF16)
             nc.sync.dma_start(out=g_in[:], in_=token_tile(grad_out, i))
-            p_in = loads.tile([PARTS, FEATURES], F32, bufs=LOADS_AHEAD + BATCH)
+            p_in = loads.tile(BY_TOKEN, F32, bufs=LOADS_AHEAD + GROUP)
             nc.sync.dma_start(out=p_in[:], in_=token_tile(p_saved, i))
-            v_in = loads.tile([PARTS, FEATURES], F32, bufs=LOADS_AHEAD + BATCH)
+            v_in = loads.tile(BY_TOKEN, F32, bufs=LOADS_AHEAD + GROUP)
             nc.sync.dma_start(out=v_in[:], in_=token_tile(v_saved, i))
             inputs[i] = (q_in, g_in, p_in, v_in)
 
         def sigmoid(i):
-            sq = by_token.tile([PARTS, FEATURES], F32)
+            sq = by_token.tile(BY_TOKEN, F32)
             nc.scalar.activation(out=sq[:], in_=inputs[i][0][:], func=FUNC.Sigmoid)
-            one_minus = by_token.tile([PARTS, FEATURES], F32, bufs=BATCH + 3)
+            one_minus = by_token.tile(BY_TOKEN, F32, bufs=GROUP + 3)
             nc.scalar.activation(out=one_minus[:], in_=inputs[i][0][:], func=FUNC.Sigmoid, scale=-1.0)
             sigmoids[i] = (sq, one_minus)
 
         def products_by_token(i):
             g_in, p_in, v_in = inputs[i][1:]
             sq = sigmoids[i][0]
-            gs = by_token.tile([PARTS, FEATURES], F32, bufs=BATCH + 2)
+            gs = by_token.tile(BY_TOKEN, F32, bufs=GROUP + 2)
             nc.vector.tensor_tensor(out=gs[:], in0=g_in[:], in1=sq[:], op=ALU.mult)
-            pv = by_token.tile([PARTS, FEATURES], F32)
+            pv = by_token.tile(BY_TOKEN, F32)
             nc.vector.tensor_tensor(out=pv[:], in0=p_in[:], in1=v_in[:], op=ALU.mult)
             products[i] = (gs, pv)
 
@@ -115,38 +125,38 @@ def tile_aftattention_t_v_kernel(
             return by_feature.tile(shape, dtype, tag="slot%d" % (i % 2), bufs=1, align_bytes=64, name="slot")
 
         def derivative(i):
-            a = shared_slot(i, [PARTS, FEATURES], F32)
+            a = shared_slot(i, BY_TOKEN, F32)
             nc.gpsimd.tensor_tensor(out=a[:], in0=products[i][0][:], in1=sigmoids[i][1][:], op=ALU.mult)
             derivatives[i] = a
 
         def add_to_sums(i):
-            half, b = divmod(i, BATCH)
-            if b == 0:
-                weighted_bank = psum_sums.tile([PARTS, PACK, PARTS], F32)
-                dw_bank = psum_sums.tile([PARTS, PACK, PARTS], F32)
-                sum_banks[half] = (weighted_bank, dw_bank)
-            for bank, source in zip(sum_banks[half], (products[i][1], products[i][0])):
-                for j in range(PACK):
-                    nc.tensor.matmul(
-                        out=bank[:, j, :],
-                        lhsT=source[:, j * BLOCK : (j + 1) * BLOCK],
-                        rhs=identity[:],
-                        is_transpose=True,
-                        start=(b == 0 and j == 0),
-                        stop=(b == BATCH - 1 and j == PACK - 1),
-                    )
-            if b == BATCH - 1:
-                weighted_bank, dw_bank = sum_banks[half]
-                weighted = by_feature.tile([PARTS, PARTS, PACK], F32, bufs=2)
-                nc.scalar.copy(out=weighted[:], in_=weighted_bank[:].rearrange("p j t -> p t j"))
-                dw = by_feature.tile([PARTS, PARTS, PACK], F32, bufs=2)
-                nc.scalar.copy(out=dw[:], in_=dw_bank[:].rearrange("p j t -> p t j"))
-                half_sums[half] = (weighted, dw)
+            group, m = divmod(i, GROUP)
+            if m == 0:
+                sum_banks[group] = psum_sums.tile([PARTS, 2, BLOCKS, PARTS], F32, name="sum_bank")
+            bank = sum_banks[group]
+            for which, source in enumerate((products[i][1], products[i][0])):
+                for c in range(ENTRIES):
+                    for j in range(BLOCKS):
+                        nc.tensor.matmul(
+                            out=bank[:, which, j, :],
+                            lhsT=source[:, c, j * PARTS : (j + 1) * PARTS],
+                            rhs=identity[:],
+                            is_transpose=True,
+                            start=(m == 0 and which == 0 and c == 0 and j == 0),
+                            stop=(m == GROUP - 1 and which == 1 and c == ENTRIES - 1 and j == BLOCKS - 1),
+                        )
+            if m == GROUP - 1:
+                weighted = by_feature.tile([PARTS, PARTS, BLOCKS], F32, bufs=2)
+                nc.scalar.copy(out=weighted[:], in_=bank[:, 0, :, :].rearrange("p j x -> p x j"))
+                dw = by_feature.tile([PARTS, PARTS, BLOCKS], F32, bufs=2)
+                nc.scalar.copy(out=dw[:], in_=bank[:, 1, :, :].rearrange("p j x -> p x j"))
+                half_sums[group] = (weighted, dw)
 
         def turn(i, what, source):
-            bank = psum_turned.tile([PARTS, PACK, PARTS], F32, tag="turned")
-            for j in range(PACK):
-                nc.tensor.transpose(bank[:, j, :], source[:, j * BLOCK : (j + 1) * BLOCK], identity[:])
+            bank = psum_turned.tile([PARTS, BLOCKS, ENTRIES, PARTS], F32, tag="turned")
+            for c in range(ENTRIES):
+                for j in range(BLOCKS):
+                    nc.tensor.transpose(bank[:, j, c, :], source[:, c, j * PARTS : (j + 1) * PARTS], identity[:])
             turned[(i, what)] = bank
 
         def turn_v(i):
@@ -159,24 +169,27 @@ def tile_aftattention_t_v_kernel(
             turn(i, "a", derivatives[i])
 
         def products_by_feature(i):
-            weighted, dw = half_sums[i // BATCH]
+            weighted, dw = half_sums[i // GROUP]
 
             def words_of(flat):
-                return flat.rearrange("p (t j) -> p t j", j=PACK)
+                return flat.rearrange("p (c x j) -> p c x j", c=ENTRIES, j=BLOCKS)
 
             def blocks_of(what):
-                return turned[(i, what)][:].rearrange("p j t -> p t j")
+                return turned[(i, what)][:].rearrange("p j c x -> p c x j")
+
+            def for_both_entries(total):
+                return total[:].unsqueeze(1).to_broadcast([PARTS, ENTRIES, PARTS, BLOCKS])
 
             grads = shared_slot(i, [PARTS, N_PRODUCTS * FEATURES], BF16)
             d_q = grads[:, 0:FEATURES]
             d_k = grads[:, FEATURES : 2 * FEATURES]
             d_v = grads[:, 2 * FEATURES : 3 * FEATURES]
             centred = by_feature.tile([PARTS, FEATURES], F32)
-            nc.vector.tensor_tensor(out=words_of(centred[:]), in0=blocks_of("v"), in1=weighted[:], op=ALU.subtract)
+            nc.vector.tensor_tensor(out=words_of(centred[:]), in0=blocks_of("v"), in1=for_both_entries(weighted), op=ALU.subtract)
             d_v_f32 = by_feature.tile([PARTS, FEATURES], F32)
-            nc.vector.tensor_tensor(out=words_of(d_v_f32[:]), in0=blocks_of("p"), in1=dw[:], op=ALU.mult)
+            nc.vector.tensor_tensor(out=words_of(d_v_f32[:]), in0=blocks_of("p"), in1=for_both_entries(dw), op=ALU.mult)
             nc.scalar.copy(out=d_v, in_=d_v_f32[:])
-            nc.vector.tensor_tensor(out=words_of(d_q), in0=blocks_of("a"), in1=weighted[:], op=ALU.mult)
+            nc.vector.tensor_tensor(out=words_of(d_q), in0=blocks_of("a"), in1=for_both_entries(weighted), op=ALU.mult)
             nc.vector.tensor_tensor(out=d_k, in0=d_v_f32[:], in1=centred[:], op=ALU.mult)
             grads_of[i] = grads
 
@@ -219,17 +232,21 @@ def tile_aftattention_t_v_kernel(
             result = results.tile([PARTS, D_IN], F32)
             for half in range(N_HALVES):
                 nc.scalar.copy(out=result[:, half * N_MOVE : (half + 1) * N_MOVE], in_=banks_of[i][half][:])
-            nc.scalar.dma_start(out=token_tile(out, i), in_=result[:])
+            group, pair = divmod(i, GROUP)
+            for c in range(ENTRIES):
+                nc.scalar.dma_start(
+                    out=out[ENTRIES * pair + c, group * STEPS : (group + 1) * STEPS, :], in_=result[c * STEPS : (c + 1) * STEPS, :]
+                )
 
         def run(stage, i):
             if 0 <= i < N_TILES:
                 stage(i)
 
-        first_round = -(BATCH + 1 + LOADS_AHEAD)
+        first_round = -(GROUP + 1 + LOADS_AHEAD)
         for k in range(first_round, N_TILES + 1):
-            run(sigmoid, k + BATCH + 1)
-            run(products_by_token, k + BATCH)
-            run(add_to_sums, k + BATCH)
+            run(sigmoid, k + GROUP + 1)
+            run(products_by_token, k + GROUP)
+            run(add_to_sums, k + GROUP)
             run(quantise, k - 1)
             run(derivative, k + 1)
             run(multiply, k - 1)
@@ -238,4 +255,4 @@ def tile_aftattention_t_v_kernel(
             run(turn_p, k + 1)
             run(turn_a, k + 1)
             run(turn_v, k + 2)
-            run(load, k + BATCH + 1 + LOADS_AHEAD)
+            run(load, k + GROUP + 1 + LOADS_AHEAD)

@@ -234,7 +234,7 @@ def tile_aftattention_t_v_kernel(
                 nc.scalar.copy(out=result[:, half * N_MOVE : (half + 1) * N_MOVE], in_=banks_of[i][half][:])
             group, pair = divmod(i, GROUP)
             for c in range(ENTRIES):
-                nc.scalar.dma_start(
+                nc.sync.dma_start(
                     out=out[ENTRIES * pair + c, group * STEPS : (group + 1) * STEPS, :], in_=result[c * STEPS : (c + 1) * STEPS, :]
                 )
 

from contextlib import ExitStack

import concourse.mybir as mybir
from concourse.masks import make_identity

F32 = mybir.dt.float32
BF16 = mybir.dt.bfloat16
U32 = mybir.dt.uint32
U8 = mybir.dt.uint8
E4M3_X4 = mybir.dt.float8_e4m3fn_x4
E5M2_X4 = mybir.dt.float8_e5m2_x4
ALU = mybir.AluOpType
FUNC = mybir.ActivationFunctionType

PARTS = 128
BATCH, TIME, D_IN, FEATURES = 8, 256, 1024, 512
N_TILES = BATCH * TIME // PARTS
ENTRIES = 2
STEPS = PARTS // ENTRIES
GROUP = BATCH // ENTRIES
N_GROUPS = N_TILES // GROUP
SPLIT = 2
PART_WIDTH = FEATURES // SPLIT
BLOCKS = PART_WIDTH // PARTS
PACK = 4
BLOCK = FEATURES // PACK
N_MOVE = 512
N_HALVES = D_IN // N_MOVE
N_PRODUCTS = 3
LOADS_AHEAD = 3

FLOPS = 2 * N_PRODUCTS * BATCH * TIME * FEATURES * D_IN
BYTES = BATCH * TIME * FEATURES * (3 * 4 + 2) + N_PRODUCTS * FEATURES * D_IN * 2 + BATCH * TIME * D_IN * 4


def token_tile(tensor, i):
    group, pair = divmod(i, GROUP)
    rows = tensor[ENTRIES * pair : ENTRIES * (pair + 1), group * STEPS : (group + 1) * STEPS, :]
    return rows.rearrange("c t (f h) -> (t f) c h", f=SPLIT)


def tile_aftattention_t_v_kernel(
    tc, x, w_q, b_q, w_k, b_k, w_v, b_v, w_bias, q_saved, p_saved, v_saved, grad_out, out
):
    nc = tc.nc
    weights = [w_q, w_k, w_v]

    with ExitStack() as ctx:
        ctx.enter_context(tc.manual_schedule())
        consts = ctx.enter_context(tc.tile_pool(name="consts", bufs=1))
        w_stage = ctx.enter_context(tc.tile_pool(name="w_stage", bufs=N_PRODUCTS))
        loads = ctx.enter_context(tc.tile_pool(name="loads", bufs=LOADS_AHEAD + 1))
        by_token = ctx.enter_context(tc.tile_pool(name="by_token", bufs=3))
        by_feature = ctx.enter_context(tc.tile_pool(name="by_feature", bufs=3))
        packed = ctx.enter_context(tc.tile_pool(name="packed", bufs=3))
        results = ctx.enter_context(tc.tile_pool(name="results", bufs=3))
        psum_sums = ctx.enter_context(tc.psum_pool(name="psum_sums", bufs=1))
        psum_turned = ctx.enter_context(tc.psum_pool(name="psum_turned", bufs=5))
        psum_out = ctx.enter_context(tc.psum_pool(name="psum_out", bufs=N_HALVES))

        w_codes = consts.tile([PARTS, N_PRODUCTS, D_IN], U32, align_bytes=64)
        w_scales = consts.tile([PARTS, N_PRODUCTS, D_IN], U8, align_bytes=64)
        w_raw = []
        for n in range(N_PRODUCTS):
            raw = w_stage.tile([PARTS, PACK, D_IN], BF16)
            nc.sync.dma_start(out=raw[:], in_=weights[n].rearrange("(j p) d -> p j d", p=PARTS))
            w_raw.append(raw)

        identity = consts.tile([PARTS, PARTS], F32)
        make_identity(nc, identity[:])

        def regroup(copy, grouped, raw, cols):
            copy(
                out=grouped[:, cols, :].rearrange("p (c i) j -> p c j i", i=4),
                in_=raw[:, :, cols].rearrange("p j (c i) -> p c j i", i=4),
            )

        w_grouped = []
        for n in range(N_PRODUCTS + 1):
            if n < N_PRODUCTS:
                grouped = w_stage.tile([PARTS, D_IN, PACK], BF16, align_bytes=64)
                regroup(nc.vector.tensor_copy, grouped, w_raw[n], slice(0, N_MOVE))
                regroup(nc.scalar.copy, grouped, w_raw[n], slice(N_MOVE, D_IN))
                w_grouped.append(grouped)
            if n > 0:
                nc.vector.quantize_mx(
                    out=w_codes[:, n - 1, :].bitcast(E4M3_X4),
                    scales=w_scales[:, n - 1, :],
                    in_=w_grouped[n - 1][:].rearrange("p d j -> p (d j)"),
                )

        inputs, sigmoids, products, sum_banks, half_sums = {}, {}, {}, {}, {}
        turned, grads_of, packed_of, banks_of, derivatives = {}, {}, {}, {}, {}

        BY_TOKEN = [PARTS, ENTRIES, PART_WIDTH]

        def load(i):
            q_in = loads.tile(BY_TOKEN, F32)
            nc.sync.dma_start(out=q_in[:], in_=token_tile(q_saved, i))
            g_in = loads.tile(BY_TOKEN, BF16)
            nc.sync.dma_start(out=g_in[:], in_=token_tile(grad_out, i))
            p_in = loads.tile(BY_TOKEN, F32, bufs=LOADS_AHEAD + GROUP)
            nc.sync.dma_start(out=p_in[:], in_=token_tile(p_saved, i))
            v_in = loads.tile(BY_TOKEN, F32, bufs=LOADS_AHEAD + GROUP)
            nc.sync.dma_start(out=v_in[:], in_=token_tile(v_saved, i))
            inputs[i] = (q_in, g_in, p_in, v_in)

        def sigmoid(i):
            sq = by_token.tile(BY_TOKEN, F32)
            nc.scalar.activation(out=sq[:], in_=inputs[i][0][:], func=FUNC.Sigmoid)
            one_minus = by_token.tile(BY_TOKEN, F32, bufs=GROUP + 3)
            nc.scalar.activation(out=one_minus[:], in_=inputs[i][0][:], func=FUNC.Sigmoid, scale=-1.0)
            sigmoids[i] = (sq, one_minus)

        def products_by_token(i):
            g_in, p_in, v_in = inputs[i][1:]
            sq = sigmoids[i][0]
            gs = by_token.tile(BY_TOKEN, F32, bufs=GROUP + 2)
            nc.vector.tensor_tensor(out=gs[:], in0=g_in[:], in1=sq[:], op=ALU.mult)
            pv = by_token.tile(BY_TOKEN, F32)
            nc.vector.tensor_tensor(out=pv[:], in0=p_in[:], in1=v_in[:], op=ALU.mult)
            products[i] = (gs, pv)

        def shared_slot(i, shape, dtype):
            return by_feature.tile(shape, dtype, tag="slot%d" % (i % 2), bufs=1, align_bytes=64, name="slot")

        def derivative(i):
            a = shared_slot(i, BY_TOKEN, F32)
            nc.gpsimd.tensor_tensor(out=a[:], in0=products[i][0][:], in1=sigmoids[i][1][:], op=ALU.mult)
            derivatives[i] = a

        def add_to_sums(i):
            group, m = divmod(i, GROUP)
            if m == 0:
                sum_banks[group] = psum_sums.tile([PARTS, 2, BLOCKS, PARTS], F32, name="sum_bank")
            bank = sum_banks[group]
            for which, source in enumerate((products[i][1], products[i][0])):
                for c in range(ENTRIES):
                    for j in range(BLOCKS):
                        nc.tensor.matmul(
                            out=bank[:, which, j, :],
                            lhsT=source[:, c, j * PARTS : (j + 1) * PARTS],
                            rhs=identity[:],
                            is_transpose=True,
                            start=(m == 0 and which == 0 and c == 0 and j == 0),
                            stop=(m == GROUP - 1 and which == 1 and c == ENTRIES - 1 and j == BLOCKS - 1),
                        )
            if m == GROUP - 1:
                weighted = by_feature.tile([PARTS, PARTS, BLOCKS], F32, bufs=2)
                nc.scalar.copy(out=weighted[:], in_=bank[:, 0, :, :].rearrange("p j x -> p x j"))
                dw = by_feature.tile([PARTS, PARTS, BLOCKS], F32, bufs=2)
                nc.scalar.copy(out=dw[:], in_=bank[:, 1, :, :].rearrange("p j x -> p x j"))
                half_sums[group] = (weighted, dw)

        def turn(i, what, source):
            bank = psum_turned.tile([PARTS, BLOCKS, ENTRIES, PARTS], F32, tag="turned")
            for c in range(ENTRIES):
                for j in range(BLOCKS):
                    nc.tensor.transpose(bank[:, j, c, :], source[:, c, j * PARTS : (j + 1) * PARTS], identity[:])
            turned[(i, what)] = bank

        def turn_v(i):
            turn(i, "v", inputs[i][3])

        def turn_p(i):
            turn(i, "p", inputs[i][2])

        def turn_a(i):
            turn(i, "a", derivatives[i])

        def products_by_feature(i):
            weighted, dw = half_sums[i // GROUP]

            def words_of(flat):
                return flat.rearrange("p (c x j) -> p c x j", c=ENTRIES, j=BLOCKS)

            def blocks_of(what):
                return turned[(i, what)][:].rearrange("p j c x -> p c x j")

            def for_both_entries(total):
                return total[:].unsqueeze(1).to_broadcast([PARTS, ENTRIES, PARTS, BLOCKS])

            grads = shared_slot(i, [PARTS, N_PRODUCTS * FEATURES], BF16)
            d_q = grads[:, 0:FEATURES]
            d_k = grads[:, FEATURES : 2 * FEATURES]
            d_v = grads[:, 2 * FEATURES : 3 * FEATURES]
            centred = by_feature.tile([PARTS, FEATURES], F32)
            nc.vector.tensor_tensor(out=words_of(centred[:]), in0=blocks_of("v"), in1=for_both_entries(weighted), op=ALU.subtract)
            d_v_f32 = by_feature.tile([PARTS, FEATURES], F32)
            nc.vector.tensor_tensor(out=words_of(d_v_f32[:]), in0=blocks_of("p"), in1=for_both_entries(dw), op=ALU.mult)
            nc.scalar.copy(out=d_v, in_=d_v_f32[:])
            nc.vector.tensor_tensor(out=words_of(d_q), in0=blocks_of("a"), in1=for_both_entries(weighted), op=ALU.mult)
            nc.vector.tensor_tensor(out=d_k, in0=d_v_f32[:], in1=centred[:], op=ALU.mult)
            grads_of[i] = grads

        def quantise(i):
            grads = grads_of[i]
            codes = packed.tile([PARTS, N_PRODUCTS * PARTS], U32, align_bytes=64)
            scales = packed.tile([PARTS, N_PRODUCTS * PARTS], U8, align_bytes=64)
            nc.vector.quantize_mx(
                out=codes[:, 0 : 2 * PARTS].bitcast(E5M2_X4),
                scales=scales[:, 0 : 2 * PARTS],
                in_=grads[:, 0 : 2 * FEATURES],
            )
            nc.vector.quantize_mx(
                out=codes[:, 2 * PARTS : 3 * PARTS].bitcast(E5M2_X4),
                scales=scales[:, 2 * PARTS : 3 * PARTS],
                in_=grads[:, 2 * FEATURES : 3 * FEATURES],
            )
            packed_of[i] = (codes, scales)

        def multiply(i):
            codes, scales = packed_of[i]
            banks_of[i] = []
            for half in range(N_HALVES):
                cols = slice(half * N_MOVE, (half + 1) * N_MOVE)
                acc = psum_out.tile([PARTS, N_MOVE], F32)
                for n in range(N_PRODUCTS):
                    tokens = slice(n * PARTS, (n + 1) * PARTS)
                    nc.tensor.matmul_mx(
                        out=acc[:],
                        lhsT=codes[:, tokens].bitcast(E5M2_X4),
                        lhsT_scale=scales[:, tokens],
                        rhs=w_codes[:, n, cols].bitcast(E4M3_X4),
                        rhs_scale=w_scales[:, n, cols],
                        start=(n == 0),
                        stop=(n == N_PRODUCTS - 1),
                    )
                banks_of[i].append(acc)

        def store(i):
            result = results.tile([PARTS, D_IN], F32)
            for half in range(N_HALVES):
                nc.scalar.copy(out=result[:, half * N_MOVE : (half + 1) * N_MOVE], in_=banks_of[i][half][:])
            group, pair = divmod(i, GROUP)
            for c in range(ENTRIES):
                nc.sync.dma_start(
                    out=out[ENTRIES * pair + c, group * STEPS : (group + 1) * STEPS, :], in_=result[c * STEPS : (c + 1) * STEPS, :]
                )

        def run(stage, i):
            if 0 <= i < N_TILES:
                stage(i)

        first_round = -(GROUP + 1 + LOADS_AHEAD)
        for k in range(first_round, N_TILES + 1):
            run(sigmoid, k + GROUP + 1)
            run(products_by_token, k + GROUP)
            run(add_to_sums, k + GROUP)
            run(quantise, k - 1)
            run(derivative, k + 1)
            run(multiply, k - 1)
            run(products_by_feature, k)
            run(store, k - 1)
            run(turn_p, k + 1)
            run(turn_a, k + 1)
            run(turn_v, k + 2)
            run(load, k + GROUP + 1 + LOADS_AHEAD)
